import numpy as np
import ml_dtypes


def mxq(x, axis, fmt="e4m3"):
    dtype, down = {"e4m3": (ml_dtypes.float8_e4m3fn, 7), "e5m2": (ml_dtypes.float8_e5m2, 14)}[fmt]
    v = np.moveaxis(np.asarray(x, np.float32).astype(ml_dtypes.bfloat16).astype(np.float64), axis, -1)
    blocks = v.reshape(v.shape[:-1] + (-1, 32))
    amax = np.abs(blocks).max(-1, keepdims=True)
    byte = np.maximum(np.where(amax > 0, np.frexp(amax)[1] - 1 + 127, 0) - down, 1)
    scale = np.exp2(byte - 127.0)
    codes = (blocks / scale).astype(np.float32).astype(dtype).astype(np.float64)
    return np.moveaxis((codes * scale).reshape(v.shape), -1, axis)


WIDE = False


def mx_kscale(k):
    if not WIDE:
        return np.ones(k)
    levels = np.array([10, -10, 5, -5, 0])
    a = np.random.permutation(np.resize(levels, k // 512 * 4)).reshape(k // 512, 4)
    idx = np.arange(k)
    return np.exp2(a[idx // 512, idx % 128 // 32])


BF16 = ml_dtypes.bfloat16


def bf(x):
    return np.asarray(x, np.float32).astype(BF16)


def f64(x):
    return np.asarray(x).astype(np.float64)


E2M1 = np.array([0.0, 0.5, 1.0, 1.5, 2.0, 3.0, 4.0, 6.0, -0.0, -0.5, -1.0, -1.5, -2.0, -3.0, -4.0, -6.0])


def pack_weight(w, fmt):
    k, n = w.shape
    w = f64(bf(w)).reshape(k // 32, 32, n)
    amax = np.abs(w).max(1)
    if fmt == "e4m3":
        byte = np.frexp(amax)[1] - 1 + 127 - 7
    else:
        mant, ex = np.frexp(amax / 6.0)
        byte = np.where(mant > 0.5, ex, ex - 1) + 127
    byte = np.clip(np.where(amax > 0, byte, 1), 1, 254)
    scaled = (w * np.exp2(127.0 - byte)[:, None, :]).reshape(k, n).astype(np.float32)
    by_word = np.ascontiguousarray(scaled.reshape(k // 512, 128, 4, n).transpose(0, 1, 3, 2))
    if fmt == "e4m3":
        words = by_word.astype(ml_dtypes.float8_e4m3fn).view(np.uint8)
    else:
        c = by_word.astype(ml_dtypes.float4_e2m1fn).view(np.uint8) & 0xF
        words = c[..., 0::2] | (c[..., 1::2] << 4)
    return np.ascontiguousarray(words), np.ascontiguousarray(byte.astype(np.uint8).reshape(k // 512, 16, n))


def unpack_weight(words, scales, fmt):
    g, p, n, _ = words.shape
    if fmt == "e4m3":
        vals = np.ascontiguousarray(words).view(ml_dtypes.float8_e4m3fn).astype(np.float64)
    else:
        nib = np.empty((g, p, n, 4), np.uint8)
        nib[..., 0::2] = words & 0xF
        nib[..., 1::2] = words >> 4
        vals = E2M1[nib]
    vals = vals * np.repeat(np.exp2(scales.astype(np.float64) - 127.0), 8, axis=1)[..., None]
    return vals.transpose(0, 1, 3, 2).reshape(g * 512, n)


B, I, H = 1024, 512, 512


def sig(v):
    return 1.0 / (1.0 + np.exp(-v))


def setup_inputs():
    s, t = mx_kscale(I), mx_kscale(H)
    x = bf(np.random.standard_normal((B, I)) * s)
    m_prev = bf(np.random.standard_normal((B, H)) * t)
    c_prev = bf(np.random.standard_normal((B, H)))
    w_m_words, w_m_scales = pack_weight(np.random.standard_normal((H, 8 * H)) / np.sqrt(H) / t[:, None], "e4m3")
    w_inputs_words, w_inputs_scales = pack_weight(np.random.standard_normal((I, 8 * H)) / np.sqrt(I) / s[:, None], "e4m3")
    return {"x": x,
            "m_prev": m_prev,
            "c_prev": c_prev,
            "w_m_words": w_m_words,
            "w_m_scales": w_m_scales,
            "w_inputs_words": w_inputs_words,
            "w_inputs_scales": w_inputs_scales}


def reference(x, m_prev, c_prev, w_m_words, w_m_scales, w_inputs_words, w_inputs_scales):
    m_mat = mxq(f64(m_prev), 1, "e4m3") @ unpack_weight(w_m_words, w_m_scales, "e4m3")
    in_mat = mxq(f64(x), 1, "e4m3") @ unpack_weight(w_inputs_words, w_inputs_scales, "e4m3")
    ms = np.split(m_mat, 8, axis=1)
    xs = np.split(in_mat, 8, axis=1)
    l1_0 = sig(xs[0] + ms[0])
    l1_1 = np.maximum(xs[1] + ms[1], 0.0)
    l1_2 = sig(xs[2] + ms[2])
    l1_3 = np.maximum(xs[3] * ms[3], 0.0)
    l1_4 = np.tanh(xs[4] + ms[4])
    l1_5 = sig(xs[5] + ms[5])
    l1_6 = np.tanh(xs[6] + ms[6])
    l1_7 = sig(xs[7] + ms[7])
    l2_0 = np.tanh(l1_0 * l1_1)
    l2_1 = np.tanh(l1_2 + l1_3)
    l2_2 = np.tanh(l1_4 * l1_5)
    l2_3 = sig(l1_6 + l1_7)
    l2_0 = np.tanh(l2_0 + f64(c_prev))
    new_c = l2_0 * l2_1
    l3_1 = np.tanh(l2_2 + l2_3)
    new_m = np.tanh(new_c * l3_1)
    return (new_m, new_c)

@@ -1,0 +1,228 @@
+from contextlib import ExitStack
+
+import concourse.mybir as mybir
+from concourse.masks import make_identity
+
+F32 = mybir.dt.float32
+BF16 = mybir.dt.bfloat16
+I32 = mybir.dt.int32
+U32 = mybir.dt.uint32
+U8 = mybir.dt.uint8
+FP8X4 = mybir.dt.float8_e4m3fn_x4
+ACT = mybir.ActivationFunctionType
+ALU = mybir.AluOpType
+
+P = 128
+B = 1024
+K = 512
+H = 512
+GATES = 8
+ROW_TILES = B // P
+G = 4
+GROUPS = ROW_TILES // G
+WORDS = K // 2
+X = 0
+M = 1
+PLANE_GATES = 4
+LIVE_VALUES = 14
+
+FLOPS = 2 * 2 * B * K * GATES * H
+
+
+def tile_nascell_kernel(
+    tc, x, m_prev, c_prev, w_m_words, w_m_scales, w_inputs_words, w_inputs_scales, out_0, out_1
+):
+    nc = tc.nc
+    with ExitStack() as ctx:
+        ctx.enter_context(tc.manual_schedule())
+        consts = ctx.enter_context(tc.tile_pool(name="consts", bufs=1))
+        weights = ctx.enter_context(tc.tile_pool(name="weights", bufs=1))
+        inputs = ctx.enter_context(tc.tile_pool(name="inputs", bufs=GROUPS))
+        staging = ctx.enter_context(tc.tile_pool(name="staging", bufs=G))
+        values = ctx.enter_context(tc.tile_pool(name="values", bufs=LIVE_VALUES))
+        psum = ctx.enter_context(tc.psum_pool(name="psum", bufs=8))
+
+        by_row_tile = "(p i) c -> p i c"
+        activations_hbm = (
+            x.rearrange(by_row_tile, i=ROW_TILES),
+            m_prev.rearrange(by_row_tile, i=ROW_TILES),
+        )
+        c_hbm = c_prev.rearrange(by_row_tile, i=ROW_TILES)
+        new_m_hbm = out_0.rearrange(by_row_tile, i=ROW_TILES)
+        new_c_hbm = out_1.rearrange(by_row_tile, i=ROW_TILES)
+        words_hbm = (
+            w_inputs_words[0].rearrange("p n t -> p (n t)").bitcast(I32),
+            w_m_words[0].rearrange("p n t -> p (n t)").bitcast(I32),
+        )
+        scales_hbm = (w_inputs_scales.bitcast(I32), w_m_scales.bitcast(I32))
+
+        identity = consts.tile([P, P], F32, name="identity")
+        w_codes = [weights.tile([P, GATES * H], U32, name="w_codes_%d" % o, align_bytes=64) for o in (X, M)]
+        w_planes = weights.tile([P, PLANE_GATES * H], U8, name="w_planes", align_bytes=64)
+        a_codes = weights.tile([P, ROW_TILES, 2, P], U32, name="a_codes", align_bytes=64)
+        a_planes = weights.tile([P, ROW_TILES, 2, P], U8, name="a_planes", align_bytes=64)
+        c_sb = weights.tile([P, ROW_TILES, H], BF16, name="c_sb")
+
+        def group_rows(h):
+            return slice(h * G, (h + 1) * G)
+
+        def gate_columns(g):
+            return slice(g * H, (g + 1) * H)
+
+        def load_activations(h):
+            loaded = []
+            for o in (X, M):
+                rows = inputs.tile([P, G, K], BF16, name="rows_%d" % o)
+                nc.sync.dma_start(out=rows[:], in_=activations_hbm[o][:, group_rows(h), :])
+                loaded.append(rows)
+            return loaded
+
+        def load_scale_rows(o):
+            for quadrant in range(4):
+                first = 32 * quadrant + 8 * o
+                nc.sync.dma_start(
+                    out=w_planes[first : first + 8, :].bitcast(I32),
+                    in_=scales_hbm[o][0, 4 * quadrant : 4 * quadrant + 4, :].rearrange(
+                        "r (half n) -> half r n", half=GATES // PLANE_GATES
+                    ),
+                )
+
+        def load_gate(g):
+            for o in (X, M):
+                nc.sync.dma_start(
+                    out=w_codes[o][:, gate_columns(g)].bitcast(I32), in_=words_hbm[o][:, gate_columns(g)]
+                )
+
+        def load_c(h):
+            nc.sync.dma_start(out=c_sb[:, group_rows(h), :], in_=c_hbm[:, group_rows(h), :])
+
+        nc.vector.memset(w_planes[:].bitcast(I32), 0)
+        make_identity(nc, identity[:])
+
+        rows_of_group = [load_activations(0)]
+        load_scale_rows(X)
+        load_scale_rows(M)
+        for g in range(GATES // 2):
+            load_gate(g)
+        load_c(0)
+        for g in range(GATES // 2, GATES):
+            load_gate(g)
+        rows_of_group.append(load_activations(1))
+        load_c(1)
+
+        def quantise(row_tile, grouped):
+            nc.vector.quantize_mx(
+                out=a_codes[:, row_tile, :, :].rearrange("p o r -> p (o r)").bitcast(FP8X4),
+                scales=a_planes[:, row_tile, :, :].rearrange("p o r -> p (o r)"),
+                in_=grouped[:].rearrange("p o r t -> p (o r t)"),
+            )
+
+        def quantise_group(h):
+            waiting = None
+            for i in range(G):
+                turned = psum.tile([P, 2, 2, P], F32, name="turned", tag="bank")
+                for o in (X, M):
+                    words = rows_of_group[h][o][:, i, :].bitcast(F32)
+                    for u in range(2):
+                        nc.tensor.transpose(turned[:, o, u, :], words[:, u:WORDS:2], identity[:])
+                grouped = staging.tile([P, 2, P, 4], BF16, name="grouped", align_bytes=64)
+                nc.vector.tensor_copy(out=grouped[:].bitcast(F32), in_=turned[:].rearrange("p o u r -> p o r u"))
+                if waiting is not None:
+                    quantise(h * G + i - 1, waiting)
+                waiting = grouped
+            quantise(h * G + G - 1, waiting)
+
+        def mx_pass(bank, o, row_tile, g, start, stop):
+            first = 8 * o + 4 * (g // PLANE_GATES)
+            nc.tensor.matmul_mx(
+                out=bank[:],
+                lhsT=a_codes[:, row_tile, o, :].bitcast(FP8X4),
+                lhsT_scale=a_planes[:, row_tile, o, :],
+                rhs=w_codes[o][:, gate_columns(g)].bitcast(FP8X4),
+                rhs_scale=w_planes[first:P, gate_columns(g % PLANE_GATES)],
+                start=start,
+                stop=stop,
+            )
+
+        def gate_sum(h, g):
+            banks = []
+            for i in range(G):
+                bank = psum.tile([P, H], F32, name="gate_sum", tag="bank")
+                mx_pass(bank, X, h * G + i, g, True, False)
+                mx_pass(bank, M, h * G + i, g, False, True)
+                banks.append(bank[:])
+            return banks
+
+        def gate_alone(h, g, o):
+            banks = []
+            for i in range(G):
+                bank = psum.tile([P, H], F32, name="gate_alone", tag="bank")
+                mx_pass(bank, o, h * G + i, g, True, True)
+                banks.append(bank[:])
+            return banks
+
+        def new_value(name):
+            value = values.tile([P, G, H], F32, name=name, tag="value")
+            return [value[:, i, :] for i in range(G)]
+
+        def activate(name, func, source):
+            out = new_value(name)
+            for i in range(G):
+                nc.scalar.activation(out=out[i], in_=source[i], func=func)
+            return out
+
+        def combine(name, op, a, b):
+            out = new_value(name)
+            for i in range(G):
+                nc.vector.tensor_tensor(out=out[i], in0=a[i], in1=b[i], op=op)
+            return out
+
+        def relu_then(name, op, a, b):
+            out = new_value(name)
+            for i in range(G):
+                nc.vector.scalar_tensor_tensor(out=out[i], in0=a[i], scalar=0.0, in1=b[i], op0=ALU.max, op1=op)
+            return out
+
+        def out_of_psum(name, banks):
+            out = new_value(name)
+            for i in range(G):
+                nc.vector.tensor_copy(out=out[i], in_=banks[i])
+            return out
+
+        def store(hbm, h, value):
+            for i in range(G):
+                nc.sync.dma_start(out=hbm[:, h * G + i, :], in_=value[i])
+
+        quantise_group(0)
+        for h in range(GROUPS):
+            c_rows = [c_sb[:, h * G + i, :] for i in range(G)]
+
+            l1_0 = activate("l1_0", ACT.Sigmoid, gate_sum(h, 0))
+            l1_0_l1_1 = relu_then("l1_0_l1_1", ALU.mult, gate_sum(h, 1), l1_0)
+            l1_2 = activate("l1_2", ACT.Sigmoid, gate_sum(h, 2))
+            l2_0_inner = activate("l2_0_inner", ACT.Tanh, l1_0_l1_1)
+            ms_3 = out_of_psum("ms_3", gate_alone(h, 3, M))
+            xs_3_ms_3 = combine("xs_3_ms_3", ALU.mult, gate_alone(h, 3, X), ms_3)
+            l1_2_l1_3 = relu_then("l1_2_l1_3", ALU.add, xs_3_ms_3, l1_2)
+            l2_0_sum = combine("l2_0_sum", ALU.add, l2_0_inner, c_rows)
+
+            l1_4 = activate("l1_4", ACT.Tanh, gate_sum(h, 4))
+            l1_5 = activate("l1_5", ACT.Sigmoid, gate_sum(h, 5))
+            l1_4_l1_5 = combine("l1_4_l1_5", ALU.mult, l1_4, l1_5)
+            l2_1 = activate("l2_1", ACT.Tanh, l1_2_l1_3)
+            l2_0 = activate("l2_0", ACT.Tanh, l2_0_sum)
+            new_c = combine("new_c", ALU.mult, l2_0, l2_1)
+            store(new_c_hbm, h, new_c)
+
+            l1_6 = activate("l1_6", ACT.Tanh, gate_sum(h, 6))
+            l1_7 = activate("l1_7", ACT.Sigmoid, gate_sum(h, 7))
+            if h + 1 < GROUPS:
+                quantise_group(h + 1)
+            l1_6_l1_7 = combine("l1_6_l1_7", ALU.add, l1_6, l1_7)
+            l2_2 = activate("l2_2", ACT.Tanh, l1_4_l1_5)
+            l2_3 = activate("l2_3", ACT.Sigmoid, l1_6_l1_7)
+            l2_2_l2_3 = combine("l2_2_l2_3", ALU.add, l2_2, l2_3)
+            l3_1 = activate("l3_1", ACT.Tanh, l2_2_l2_3)
+            new_c_l3_1 = combine("new_c_l3_1", ALU.mult, new_c, l3_1)
+            new_m = activate("new_m", ACT.Tanh, new_c_l3_1)
+            store(new_m_hbm, h, new_m)

@@ -18,13 +18,14 @@ K = 512
 H = 512
 GATES = 8
 ROW_TILES = B // P
-G = 4
+G = 2
 GROUPS = ROW_TILES // G
 WORDS = K // 2
 X = 0
 M = 1
+GATE_ORDER = (6, 7, 0, 1, 4, 3, 5, 2)
 PLANE_GATES = 4
-LIVE_VALUES = 14
+LIVE_VALUES = 24
 
 FLOPS = 2 * 2 * B * K * GATES * H
 
@@ -38,7 +39,7 @@ def tile_nascell_kernel(
         consts = ctx.enter_context(tc.tile_pool(name="consts", bufs=1))
         weights = ctx.enter_context(tc.tile_pool(name="weights", bufs=1))
         inputs = ctx.enter_context(tc.tile_pool(name="inputs", bufs=GROUPS))
-        staging = ctx.enter_context(tc.tile_pool(name="staging", bufs=G))
+        staging = ctx.enter_context(tc.tile_pool(name="staging", bufs=2 * G))
         values = ctx.enter_context(tc.tile_pool(name="values", bufs=LIVE_VALUES))
         psum = ctx.enter_context(tc.psum_pool(name="psum", bufs=8))
 
@@ -102,13 +103,16 @@ def tile_nascell_kernel(
         rows_of_group = [load_activations(0)]
         load_scale_rows(X)
         load_scale_rows(M)
-        for g in range(GATES // 2):
+        for g in GATE_ORDER[: GATES // 2]:
             load_gate(g)
         load_c(0)
-        for g in range(GATES // 2, GATES):
-            load_gate(g)
         rows_of_group.append(load_activations(1))
-        load_c(1)
+        for g in GATE_ORDER[GATES // 2 :]:
+            load_gate(g)
+        for h in range(1, GROUPS):
+            load_c(h)
+            if h + 1 < GROUPS:
+                rows_of_group.append(load_activations(h + 1))
 
         def quantise(row_tile, grouped):
             nc.vector.quantize_mx(
@@ -193,36 +197,39 @@ def tile_nascell_kernel(
             for i in range(G):
                 nc.sync.dma_start(out=hbm[:, h * G + i, :], in_=value[i])
 
+        def finish(h, new_c_l3_1):
+            new_m = activate("new_m", ACT.Tanh, new_c_l3_1)
+            store(new_m_hbm, h, new_m)
+
         quantise_group(0)
         for h in range(GROUPS):
             c_rows = [c_sb[:, h * G + i, :] for i in range(G)]
 
-            l1_0 = activate("l1_0", ACT.Sigmoid, gate_sum(h, 0))
-            l1_0_l1_1 = relu_then("l1_0_l1_1", ALU.mult, gate_sum(h, 1), l1_0)
-            l1_2 = activate("l1_2", ACT.Sigmoid, gate_sum(h, 2))
-            l2_0_inner = activate("l2_0_inner", ACT.Tanh, l1_0_l1_1)
-            ms_3 = out_of_psum("ms_3", gate_alone(h, 3, M))
-            xs_3_ms_3 = combine("xs_3_ms_3", ALU.mult, gate_alone(h, 3, X), ms_3)
-            l1_2_l1_3 = relu_then("l1_2_l1_3", ALU.add, xs_3_ms_3, l1_2)
-            l2_0_sum = combine("l2_0_sum", ALU.add, l2_0_inner, c_rows)
-
-            l1_4 = activate("l1_4", ACT.Tanh, gate_sum(h, 4))
-            l1_5 = activate("l1_5", ACT.Sigmoid, gate_sum(h, 5))
-            l1_4_l1_5 = combine("l1_4_l1_5", ALU.mult, l1_4, l1_5)
-            l2_1 = activate("l2_1", ACT.Tanh, l1_2_l1_3)
-            l2_0 = activate("l2_0", ACT.Tanh, l2_0_sum)
-            new_c = combine("new_c", ALU.mult, l2_0, l2_1)
-            store(new_c_hbm, h, new_c)
-
             l1_6 = activate("l1_6", ACT.Tanh, gate_sum(h, 6))
+            if h > 0:
+                finish(h - 1, new_c_l3_1)
             l1_7 = activate("l1_7", ACT.Sigmoid, gate_sum(h, 7))
+            l1_6_l1_7 = combine("l1_6_l1_7", ALU.add, l1_6, l1_7)
+            l1_0 = activate("l1_0", ACT.Sigmoid, gate_sum(h, 0))
+            l2_3 = activate("l2_3", ACT.Sigmoid, l1_6_l1_7)
+            l1_0_l1_1 = relu_then("l1_0_l1_1", ALU.mult, gate_sum(h, 1), l1_0)
             if h + 1 < GROUPS:
                 quantise_group(h + 1)
-            l1_6_l1_7 = combine("l1_6_l1_7", ALU.add, l1_6, l1_7)
+            l2_0_inner = activate("l2_0_inner", ACT.Tanh, l1_0_l1_1)
+            l1_4 = activate("l1_4", ACT.Tanh, gate_sum(h, 4))
+            l2_0_sum = combine("l2_0_sum", ALU.add, l2_0_inner, c_rows)
+            l2_0 = activate("l2_0", ACT.Tanh, l2_0_sum)
+            ms_3 = out_of_psum("ms_3", gate_alone(h, 3, M))
+            xs_3_ms_3 = combine("xs_3_ms_3", ALU.mult, gate_alone(h, 3, X), ms_3)
+            l1_5 = activate("l1_5", ACT.Sigmoid, gate_sum(h, 5))
+            l1_4_l1_5 = combine("l1_4_l1_5", ALU.mult, l1_4, l1_5)
+            l1_2 = activate("l1_2", ACT.Sigmoid, gate_sum(h, 2))
+            l1_2_l1_3 = relu_then("l1_2_l1_3", ALU.add, xs_3_ms_3, l1_2)
             l2_2 = activate("l2_2", ACT.Tanh, l1_4_l1_5)
-            l2_3 = activate("l2_3", ACT.Sigmoid, l1_6_l1_7)
             l2_2_l2_3 = combine("l2_2_l2_3", ALU.add, l2_2, l2_3)
+            l2_1 = activate("l2_1", ACT.Tanh, l1_2_l1_3)
+            new_c = combine("new_c", ALU.mult, l2_0, l2_1)
+            store(new_c_hbm, h, new_c)
             l3_1 = activate("l3_1", ACT.Tanh, l2_2_l2_3)
             new_c_l3_1 = combine("new_c_l3_1", ALU.mult, new_c, l3_1)
-            new_m = activate("new_m", ACT.Tanh, new_c_l3_1)
-            store(new_m_hbm, h, new_m)
+        finish(GROUPS - 1, new_c_l3_1)

@@ -23,7 +23,7 @@ GROUPS = ROW_TILES // G
 WORDS = K // 2
 X = 0
 M = 1
-GATE_ORDER = (6, 7, 0, 1, 4, 3, 5, 2)
+GATE_ORDER = (7, 6, 0, 1, 4, 3, 5, 2)
 PLANE_GATES = 4
 LIVE_VALUES = 24
 
@@ -205,10 +205,10 @@ def tile_nascell_kernel(
         for h in range(GROUPS):
             c_rows = [c_sb[:, h * G + i, :] for i in range(G)]
 
-            l1_6 = activate("l1_6", ACT.Tanh, gate_sum(h, 6))
+            l1_7 = activate("l1_7", ACT.Sigmoid, gate_sum(h, 7))
             if h > 0:
                 finish(h - 1, new_c_l3_1)
-            l1_7 = activate("l1_7", ACT.Sigmoid, gate_sum(h, 7))
+            l1_6 = activate("l1_6", ACT.Tanh, gate_sum(h, 6))
             l1_6_l1_7 = combine("l1_6_l1_7", ALU.add, l1_6, l1_7)
             l1_0 = activate("l1_0", ACT.Sigmoid, gate_sum(h, 0))
             l2_3 = activate("l2_3", ACT.Sigmoid, l1_6_l1_7)

@@ -24,7 +24,8 @@ WORDS = K // 2
 X = 0
 M = 1
 GATE_ORDER = (7, 6, 0, 1, 4, 3, 5, 2)
-PLANE_GATES = 4
+PLANE_GATES = 2
+PLANES = GATES // PLANE_GATES
 LIVE_VALUES = 24
 
 FLOPS = 2 * 2 * B * K * GATES * H
@@ -59,7 +60,7 @@ def tile_nascell_kernel(
 
         identity = consts.tile([P, P], F32, name="identity")
         w_codes = [weights.tile([P, GATES * H], U32, name="w_codes_%d" % o, align_bytes=64) for o in (X, M)]
-        w_planes = weights.tile([P, PLANE_GATES * H], U8, name="w_planes", align_bytes=64)
+        w_planes = [weights.tile([P, PLANE_GATES * H], U8, name="w_planes_%d" % o, align_bytes=64) for o in (X, M)]
         a_codes = weights.tile([P, ROW_TILES, 2, P], U32, name="a_codes", align_bytes=64)
         a_planes = weights.tile([P, ROW_TILES, 2, P], U8, name="a_planes", align_bytes=64)
         c_sb = weights.tile([P, ROW_TILES, H], BF16, name="c_sb")
@@ -70,23 +71,22 @@ def tile_nascell_kernel(
         def gate_columns(g):
             return slice(g * H, (g + 1) * H)
 
-        def load_activations(h):
+        def load_activations(h, queue):
             loaded = []
             for o in (X, M):
                 rows = inputs.tile([P, G, K], BF16, name="rows_%d" % o)
-                nc.sync.dma_start(out=rows[:], in_=activations_hbm[o][:, group_rows(h), :])
+                queue.dma_start(out=rows[:], in_=activations_hbm[o][:, group_rows(h), :])
                 loaded.append(rows)
             return loaded
 
         def load_scale_rows(o):
             for quadrant in range(4):
-                first = 32 * quadrant + 8 * o
+                first = 32 * quadrant
                 nc.sync.dma_start(
-                    out=w_planes[first : first + 8, :].bitcast(I32),
-                    in_=scales_hbm[o][0, 4 * quadrant : 4 * quadrant + 4, :].rearrange(
-                        "r (half n) -> half r n", half=GATES // PLANE_GATES
-                    ),
+                    out=w_planes[o][first : first + 4 * PLANES, :].bitcast(I32),
+                    in_=scales_hbm[o][0, 4 * quadrant : 4 * quadrant + 4, :].rearrange("r (j n) -> j r n", j=PLANES),
                 )
+
 
         def load_gate(g):
             for o in (X, M):
@@ -97,22 +97,24 @@ def tile_nascell_kernel(
         def load_c(h):
             nc.sync.dma_start(out=c_sb[:, group_rows(h), :], in_=c_hbm[:, group_rows(h), :])
 
-        nc.vector.memset(w_planes[:].bitcast(I32), 0)
+        for o in (X, M):
+            nc.vector.memset(w_planes[o][:].bitcast(I32), 0)
         make_identity(nc, identity[:])
 
-        rows_of_group = [load_activations(0)]
+        rows_of_group = [load_activations(0, nc.scalar)]
         load_scale_rows(X)
+        load_gate(GATE_ORDER[0])
         load_scale_rows(M)
-        for g in GATE_ORDER[: GATES // 2]:
+        for g in GATE_ORDER[1 : GATES // 2]:
             load_gate(g)
         load_c(0)
-        rows_of_group.append(load_activations(1))
+        rows_of_group.append(load_activations(1, nc.sync))
         for g in GATE_ORDER[GATES // 2 :]:
             load_gate(g)
         for h in range(1, GROUPS):
             load_c(h)
             if h + 1 < GROUPS:
-                rows_of_group.append(load_activations(h + 1))
+                rows_of_group.append(load_activations(h + 1, nc.sync))
 
         def quantise(row_tile, grouped):
             nc.vector.quantize_mx(
@@ -136,14 +138,42 @@ def tile_nascell_kernel(
                 waiting = grouped
             quantise(h * G + G - 1, waiting)
 
+        def quantise_first_group():
+            for o in (X, M):
+                turned = []
+                for i in range(G):
+                    bank = psum.tile([P, 2, P], F32, name="turned_one", tag="bank")
+                    words = rows_of_group[0][o][:, i, :].bitcast(F32)
+                    for u in range(2):
+                        nc.tensor.transpose(bank[:, u, :], words[:, u:WORDS:2], identity[:])
+                    turned.append(bank)
+                grouped = []
+                for i in range(G):
+                    pairs = staging.tile([P, P, 4], BF16, name="grouped_one", align_bytes=64)
+                    grouped.append(pairs)
+                steps = [("copy", 0), ("copy", 1), ("quantise", 0), ("quantise", 1)]
+                if o == M:
+                    steps = [("copy", 0), ("quantise", 0), ("copy", 1), ("quantise", 1)]
+                for step, i in steps:
+                    if step == "copy":
+                        nc.vector.tensor_copy(
+                            out=grouped[i][:].bitcast(F32), in_=turned[i][:].rearrange("p u r -> p r u")
+                        )
+                    else:
+                        nc.vector.quantize_mx(
+                            out=a_codes[:, i, o, :].bitcast(FP8X4),
+                            scales=a_planes[:, i, o, :],
+                            in_=grouped[i][:].rearrange("p r t -> p (r t)"),
+                        )
+
         def mx_pass(bank, o, row_tile, g, start, stop):
-            first = 8 * o + 4 * (g // PLANE_GATES)
+            first = 4 * (g // PLANE_GATES)
             nc.tensor.matmul_mx(
                 out=bank[:],
                 lhsT=a_codes[:, row_tile, o, :].bitcast(FP8X4),
                 lhsT_scale=a_planes[:, row_tile, o, :],
                 rhs=w_codes[o][:, gate_columns(g)].bitcast(FP8X4),
-                rhs_scale=w_planes[first:P, gate_columns(g % PLANE_GATES)],
+                rhs_scale=w_planes[o][first:P, gate_columns(g % PLANE_GATES)],
                 start=start,
                 stop=stop,
             )
@@ -201,7 +231,7 @@ def tile_nascell_kernel(
             new_m = activate("new_m", ACT.Tanh, new_c_l3_1)
             store(new_m_hbm, h, new_m)
 
-        quantise_group(0)
+        quantise_first_group()
         for h in range(GROUPS):
             c_rows = [c_sb[:, h * G + i, :] for i in range(G)]
 

@@ -195,37 +195,45 @@ def tile_nascell_kernel(
                 banks.append(bank[:])
             return banks
 
-        def new_value(name):
-            value = values.tile([P, G, H], F32, name=name, tag="value")
-            return [value[:, i, :] for i in range(G)]
+        def pieces_of(flat, pieces):
+            width = G * H // pieces
+            return [flat[:, j * width : (j + 1) * width] for j in range(pieces)]
+
+        def halves(views):
+            return [view[:, c : c + view.shape[1] // 2] for view in views for c in (0, view.shape[1] // 2)]
+
+        def new_value(name, pieces):
+            value = values.tile([P, G * H], F32, name=name, tag="value")
+            return pieces_of(value, pieces)
 
         def activate(name, func, source):
-            out = new_value(name)
-            for i in range(G):
-                nc.scalar.activation(out=out[i], in_=source[i], func=func)
+            out = new_value(name, len(source))
+            for j in range(len(source)):
+                nc.scalar.activation(out=out[j], in_=source[j], func=func)
             return out
 
         def combine(name, op, a, b):
-            out = new_value(name)
-            for i in range(G):
-                nc.vector.tensor_tensor(out=out[i], in0=a[i], in1=b[i], op=op)
+            out = new_value(name, len(a))
+            for j in range(len(a)):
+                nc.vector.tensor_tensor(out=out[j], in0=a[j], in1=b[j], op=op)
             return out
 
         def relu_then(name, op, a, b):
-            out = new_value(name)
-            for i in range(G):
-                nc.vector.scalar_tensor_tensor(out=out[i], in0=a[i], scalar=0.0, in1=b[i], op0=ALU.max, op1=op)
+            out = new_value(name, len(a))
+            for j in range(len(a)):
+                nc.vector.scalar_tensor_tensor(out=out[j], in0=a[j], scalar=0.0, in1=b[j], op0=ALU.max, op1=op)
             return out
 
         def out_of_psum(name, banks):
-            out = new_value(name)
-            for i in range(G):
-                nc.vector.tensor_copy(out=out[i], in_=banks[i])
+            out = new_value(name, len(banks))
+            for j in range(len(banks)):
+                nc.vector.tensor_copy(out=out[j], in_=banks[j])
             return out
 
         def store(hbm, h, value):
-            for i in range(G):
-                nc.sync.dma_start(out=hbm[:, h * G + i, :], in_=value[i])
+            rows = hbm[:, group_rows(h), :].rearrange("p i c -> p (i c)")
+            for part, view in zip(pieces_of(rows, len(value)), value):
+                nc.sync.dma_start(out=part, in_=view)
 
         def finish(h, new_c_l3_1):
             new_m = activate("new_m", ACT.Tanh, new_c_l3_1)
@@ -233,7 +241,7 @@ def tile_nascell_kernel(
 
         quantise_first_group()
         for h in range(GROUPS):
-            c_rows = [c_sb[:, h * G + i, :] for i in range(G)]
+            c_rows = pieces_of(c_sb[:, group_rows(h), :].rearrange("p i c -> p (i c)"), G)
 
             l1_7 = activate("l1_7", ACT.Sigmoid, gate_sum(h, 7))
             if h > 0:
@@ -260,6 +268,8 @@ def tile_nascell_kernel(
             l2_1 = activate("l2_1", ACT.Tanh, l1_2_l1_3)
             new_c = combine("new_c", ALU.mult, l2_0, l2_1)
             store(new_c_hbm, h, new_c)
+            if h == GROUPS - 1:
+                l2_2_l2_3, new_c = halves(l2_2_l2_3), halves(new_c)
             l3_1 = activate("l3_1", ACT.Tanh, l2_2_l2_3)
             new_c_l3_1 = combine("new_c_l3_1", ALU.mult, new_c, l3_1)
         finish(GROUPS - 1, new_c_l3_1)

from contextlib import ExitStack

import concourse.mybir as mybir
from concourse.masks import make_identity

F32 = mybir.dt.float32
BF16 = mybir.dt.bfloat16
I32 = mybir.dt.int32
U32 = mybir.dt.uint32
U8 = mybir.dt.uint8
FP8X4 = mybir.dt.float8_e4m3fn_x4
ACT = mybir.ActivationFunctionType
ALU = mybir.AluOpType

P = 128
B = 1024
K = 512
H = 512
GATES = 8
ROW_TILES = B // P
G = 2
GROUPS = ROW_TILES // G
WORDS = K // 2
X = 0
M = 1
GATE_ORDER = (7, 6, 0, 1, 4, 3, 5, 2)
PLANE_GATES = 2
PLANES = GATES // PLANE_GATES
LIVE_VALUES = 24

FLOPS = 2 * 2 * B * K * GATES * H


def tile_nascell_kernel(
    tc, x, m_prev, c_prev, w_m_words, w_m_scales, w_inputs_words, w_inputs_scales, out_0, out_1
):
    nc = tc.nc
    with ExitStack() as ctx:
        ctx.enter_context(tc.manual_schedule())
        consts = ctx.enter_context(tc.tile_pool(name="consts", bufs=1))
        weights = ctx.enter_context(tc.tile_pool(name="weights", bufs=1))
        inputs = ctx.enter_context(tc.tile_pool(name="inputs", bufs=GROUPS))
        staging = ctx.enter_context(tc.tile_pool(name="staging", bufs=2 * G))
        values = ctx.enter_context(tc.tile_pool(name="values", bufs=LIVE_VALUES))
        psum = ctx.enter_context(tc.psum_pool(name="psum", bufs=8))

        by_row_tile = "(p i) c -> p i c"
        activations_hbm = (
            x.rearrange(by_row_tile, i=ROW_TILES),
            m_prev.rearrange(by_row_tile, i=ROW_TILES),
        )
        c_hbm = c_prev.rearrange(by_row_tile, i=ROW_TILES)
        new_m_hbm = out_0.rearrange(by_row_tile, i=ROW_TILES)
        new_c_hbm = out_1.rearrange(by_row_tile, i=ROW_TILES)
        words_hbm = (
            w_inputs_words[0].rearrange("p n t -> p (n t)").bitcast(I32),
            w_m_words[0].rearrange("p n t -> p (n t)").bitcast(I32),
        )
        scales_hbm = (w_inputs_scales.bitcast(I32), w_m_scales.bitcast(I32))

        identity = consts.tile([P, P], F32, name="identity")
        w_codes = [weights.tile([P, GATES * H], U32, name="w_codes_%d" % o, align_bytes=64) for o in (X, M)]
        w_planes = [weights.tile([P, PLANE_GATES * H], U8, name="w_planes_%d" % o, align_bytes=64) for o in (X, M)]
        a_codes = weights.tile([P, ROW_TILES, 2, P], U32, name="a_codes", align_bytes=64)
        a_planes = weights.tile([P, ROW_TILES, 2, P], U8, name="a_planes", align_bytes=64)
        c_sb = weights.tile([P, ROW_TILES, H], BF16, name="c_sb")

        def group_rows(h):
            return slice(h * G, (h + 1) * G)

        def gate_columns(g):
            return slice(g * H, (g + 1) * H)

        def load_activations(h, queue):
            loaded = []
            for o in (X, M):
                rows = inputs.tile([P, G, K], BF16, name="rows_%d" % o)
                queue.dma_start(out=rows[:], in_=activations_hbm[o][:, group_rows(h), :])
                loaded.append(rows)
            return loaded

        def load_scale_rows(o):
            for quadrant in range(4):
                first = 32 * quadrant
                nc.sync.dma_start(
                    out=w_planes[o][first : first + 4 * PLANES, :].bitcast(I32),
                    in_=scales_hbm[o][0, 4 * quadrant : 4 * quadrant + 4, :].rearrange("r (j n) -> j r n", j=PLANES),
                )


        def load_gate(g):
            for o in (X, M):
                nc.sync.dma_start(
                    out=w_codes[o][:, gate_columns(g)].bitcast(I32), in_=words_hbm[o][:, gate_columns(g)]
                )

        def load_c(h):
            nc.sync.dma_start(out=c_sb[:, group_rows(h), :], in_=c_hbm[:, group_rows(h), :])

        for o in (X, M):
            nc.vector.memset(w_planes[o][:].bitcast(I32), 0)
        make_identity(nc, identity[:])

        rows_of_group = [load_activations(0, nc.scalar)]
        load_scale_rows(X)
        load_gate(GATE_ORDER[0])
        load_scale_rows(M)
        for g in GATE_ORDER[1 : GATES // 2]:
            load_gate(g)
        load_c(0)
        rows_of_group.append(load_activations(1, nc.sync))
        for g in GATE_ORDER[GATES // 2 :]:
            load_gate(g)
        for h in range(1, GROUPS):
            load_c(h)
            if h + 1 < GROUPS:
                rows_of_group.append(load_activations(h + 1, nc.sync))

        def quantise(row_tile, grouped):
            nc.vector.quantize_mx(
                out=a_codes[:, row_tile, :, :].rearrange("p o r -> p (o r)").bitcast(FP8X4),
                scales=a_planes[:, row_tile, :, :].rearrange("p o r -> p (o r)"),
                in_=grouped[:].rearrange("p o r t -> p (o r t)"),
            )

        def quantise_group(h):
            waiting = None
            for i in range(G):
                turned = psum.tile([P, 2, 2, P], F32, name="turned", tag="bank")
                for o in (X, M):
                    words = rows_of_group[h][o][:, i, :].bitcast(F32)
                    for u in range(2):
                        nc.tensor.transpose(turned[:, o, u, :], words[:, u:WORDS:2], identity[:])
                grouped = staging.tile([P, 2, P, 4], BF16, name="grouped", align_bytes=64)
                nc.vector.tensor_copy(out=grouped[:].bitcast(F32), in_=turned[:].rearrange("p o u r -> p o r u"))
                if waiting is not None:
                    quantise(h * G + i - 1, waiting)
                waiting = grouped
            quantise(h * G + G - 1, waiting)

        def quantise_first_group():
            for o in (X, M):
                turned = []
                for i in range(G):
                    bank = psum.tile([P, 2, P], F32, name="turned_one", tag="bank")
                    words = rows_of_group[0][o][:, i, :].bitcast(F32)
                    for u in range(2):
                        nc.tensor.transpose(bank[:, u, :], words[:, u:WORDS:2], identity[:])
                    turned.append(bank)
                grouped = []
                for i in range(G):
                    pairs = staging.tile([P, P, 4], BF16, name="grouped_one", align_bytes=64)
                    grouped.append(pairs)
                steps = [("copy", 0), ("copy", 1), ("quantise", 0), ("quantise", 1)]
                if o == M:
                    steps = [("copy", 0), ("quantise", 0), ("copy", 1), ("quantise", 1)]
                for step, i in steps:
                    if step == "copy":
                        nc.vector.tensor_copy(
                            out=grouped[i][:].bitcast(F32), in_=turned[i][:].rearrange("p u r -> p r u")
                        )
                    else:
                        nc.vector.quantize_mx(
                            out=a_codes[:, i, o, :].bitcast(FP8X4),
                            scales=a_planes[:, i, o, :],
                            in_=grouped[i][:].rearrange("p r t -> p (r t)"),
                        )

        def mx_pass(bank, o, row_tile, g, start, stop):
            first = 4 * (g // PLANE_GATES)
            nc.tensor.matmul_mx(
                out=bank[:],
                lhsT=a_codes[:, row_tile, o, :].bitcast(FP8X4),
                lhsT_scale=a_planes[:, row_tile, o, :],
                rhs=w_codes[o][:, gate_columns(g)].bitcast(FP8X4),
                rhs_scale=w_planes[o][first:P, gate_columns(g % PLANE_GATES)],
                start=start,
                stop=stop,
            )

        def gate_sum(h, g):
            banks = []
            for i in range(G):
                bank = psum.tile([P, H], F32, name="gate_sum", tag="bank")
                mx_pass(bank, X, h * G + i, g, True, False)
                mx_pass(bank, M, h * G + i, g, False, True)
                banks.append(bank[:])
            return banks

        def gate_alone(h, g, o):
            banks = []
            for i in range(G):
                bank = psum.tile([P, H], F32, name="gate_alone", tag="bank")
                mx_pass(bank, o, h * G + i, g, True, True)
                banks.append(bank[:])
            return banks

        def pieces_of(flat, pieces):
            width = G * H // pieces
            return [flat[:, j * width : (j + 1) * width] for j in range(pieces)]

        def halves(views):
            return [view[:, c : c + view.shape[1] // 2] for view in views for c in (0, view.shape[1] // 2)]

        def new_value(name, pieces):
            value = values.tile([P, G * H], F32, name=name, tag="value")
            return pieces_of(value, pieces)

        def activate(name, func, source):
            out = new_value(name, len(source))
            for j in range(len(source)):
                nc.scalar.activation(out=out[j], in_=source[j], func=func)
            return out

        def combine(name, op, a, b):
            out = new_value(name, len(a))
            for j in range(len(a)):
                nc.vector.tensor_tensor(out=out[j], in0=a[j], in1=b[j], op=op)
            return out

        def relu_then(name, op, a, b):
            out = new_value(name, len(a))
            for j in range(len(a)):
                nc.vector.scalar_tensor_tensor(out=out[j], in0=a[j], scalar=0.0, in1=b[j], op0=ALU.max, op1=op)
            return out

        def out_of_psum(name, banks):
            out = new_value(name, len(banks))
            for j in range(len(banks)):
                nc.vector.tensor_copy(out=out[j], in_=banks[j])
            return out

        def store(hbm, h, value):
            rows = hbm[:, group_rows(h), :].rearrange("p i c -> p (i c)")
            for part, view in zip(pieces_of(rows, len(value)), value):
                nc.sync.dma_start(out=part, in_=view)

        def finish(h, new_c_l3_1):
            new_m = activate("new_m", ACT.Tanh, new_c_l3_1)
            store(new_m_hbm, h, new_m)

        quantise_first_group()
        for h in range(GROUPS):
            c_rows = pieces_of(c_sb[:, group_rows(h), :].rearrange("p i c -> p (i c)"), G)

            l1_7 = activate("l1_7", ACT.Sigmoid, gate_sum(h, 7))
            if h > 0:
                finish(h - 1, new_c_l3_1)
            l1_6 = activate("l1_6", ACT.Tanh, gate_sum(h, 6))
            l1_6_l1_7 = combine("l1_6_l1_7", ALU.add, l1_6, l1_7)
            l1_0 = activate("l1_0", ACT.Sigmoid, gate_sum(h, 0))
            l2_3 = activate("l2_3", ACT.Sigmoid, l1_6_l1_7)
            l1_0_l1_1 = relu_then("l1_0_l1_1", ALU.mult, gate_sum(h, 1), l1_0)
            if h + 1 < GROUPS:
                quantise_group(h + 1)
            l2_0_inner = activate("l2_0_inner", ACT.Tanh, l1_0_l1_1)
            l1_4 = activate("l1_4", ACT.Tanh, gate_sum(h, 4))
            l2_0_sum = combine("l2_0_sum", ALU.add, l2_0_inner, c_rows)
            l2_0 = activate("l2_0", ACT.Tanh, l2_0_sum)
            ms_3 = out_of_psum("ms_3", gate_alone(h, 3, M))
            xs_3_ms_3 = combine("xs_3_ms_3", ALU.mult, gate_alone(h, 3, X), ms_3)
            l1_5 = activate("l1_5", ACT.Sigmoid, gate_sum(h, 5))
            l1_4_l1_5 = combine("l1_4_l1_5", ALU.mult, l1_4, l1_5)
            l1_2 = activate("l1_2", ACT.Sigmoid, gate_sum(h, 2))
            l1_2_l1_3 = relu_then("l1_2_l1_3", ALU.add, xs_3_ms_3, l1_2)
            l2_2 = activate("l2_2", ACT.Tanh, l1_4_l1_5)
            l2_2_l2_3 = combine("l2_2_l2_3", ALU.add, l2_2, l2_3)
            l2_1 = activate("l2_1", ACT.Tanh, l1_2_l1_3)
            new_c = combine("new_c", ALU.mult, l2_0, l2_1)
            store(new_c_hbm, h, new_c)
            if h == GROUPS - 1:
                l2_2_l2_3, new_c = halves(l2_2_l2_3), halves(new_c)
            l3_1 = activate("l3_1", ACT.Tanh, l2_2_l2_3)
            new_c_l3_1 = combine("new_c_l3_1", ALU.mult, new_c, l3_1)
        finish(GROUPS - 1, new_c_l3_1)
